import numpy as np
import ml_dtypes


def mxq(x, axis, fmt="e4m3"):
    dtype, down = {"e4m3": (ml_dtypes.float8_e4m3fn, 7), "e5m2": (ml_dtypes.float8_e5m2, 14)}[fmt]
    v = np.moveaxis(np.asarray(x, np.float32).astype(ml_dtypes.bfloat16).astype(np.float64), axis, -1)
    blocks = v.reshape(v.shape[:-1] + (-1, 32))
    amax = np.abs(blocks).max(-1, keepdims=True)
    byte = np.maximum(np.where(amax > 0, np.frexp(amax)[1] - 1 + 127, 0) - down, 1)
    scale = np.exp2(byte - 127.0)
    codes = (blocks / scale).astype(np.float32).astype(dtype).astype(np.float64)
    return np.moveaxis((codes * scale).reshape(v.shape), -1, axis)


WIDE = False


def mx_kscale(k):
    if not WIDE:
        return np.ones(k)
    levels = np.array([10, -10, 5, -5, 0])
    a = np.random.permutation(np.resize(levels, k // 512 * 4)).reshape(k // 512, 4)
    idx = np.arange(k)
    return np.exp2(a[idx // 512, idx % 128 // 32])


BF16 = ml_dtypes.bfloat16


def bf(x):
    return np.asarray(x, np.float32).astype(BF16)


def f64(x):
    return np.asarray(x).astype(np.float64)


N, B, T, C, R, O, NC, H, W = 1, 128, 4, 2048, 4, 512, 512, 16, 4
K = C * R
LEAKY_SLOPE = 0.01


def setup_inputs():
    s = mx_kscale(K)
    return {"pooled": bf((0.65 + 0.3 * np.random.standard_normal((N, B, K))) * s),
            "p": bf(0.65 + 0.5 * np.random.standard_normal((N, B, T, C))),
            "Wout": bf((4.0 / np.sqrt(K) * np.random.standard_normal((N, K, C)) - 4.0 / K) / s[None, :, None])}


def reference(pooled, p, Wout):
    y = mxq(f64(pooled), 2, "e4m3") @ mxq(f64(Wout), 1, "e4m3")
    y = np.where(y >= 0, y, LEAKY_SLOPE * y)
    return np.max(f64(p) + y[:, :, None, :], axis=2)

@@ -1,0 +1,136 @@
+from contextlib import ExitStack
+
+import concourse.mybir as mybir
+from concourse.masks import make_identity
+
+BF16 = mybir.dt.bfloat16
+F32 = mybir.dt.float32
+U32 = mybir.dt.uint32
+U8 = mybir.dt.uint8
+FP8X4 = mybir.dt.float8_e4m3fn_x4
+
+P = 128
+PACK = 4
+K_PASS = P * PACK
+K = 8192
+C = 2048
+FRAMES = 4
+PASSES = K // K_PASS
+BANK = 512
+BANKS = C // BANK
+HALF = C // 2
+RUN = 4
+ROW = PACK * C
+LEAKY_SLOPE = 0.01
+
+FLOPS = 2 * P * K * C
+
+
+def regroup(copy, raw, grouped, cols):
+    src = raw.rearrange("q (j c) -> q j c", j=PACK)[:, :, cols]
+    dst = grouped.rearrange("q (c j) -> q c j", j=PACK)[:, cols, :]
+    copy(
+        out=dst.rearrange("q (n i) j -> q n j i", i=RUN),
+        in_=src.rearrange("q j (n i) -> q n j i", i=RUN),
+    )
+
+
+def quantise(nc, grouped, codes, scales, first):
+    nc.vector.quantize_mx(
+        out=codes[:, first : first + HALF].bitcast(FP8X4),
+        scales=scales[:, first : first + HALF],
+        in_=grouped[:, PACK * first : PACK * (first + HALF)],
+    )
+
+
+def tile_gmpahead_pa_k_kernel(tc, pooled, p, Wout, out):
+    nc = tc.nc
+    w_passes = Wout.rearrange("n (g q j) c -> (n g) q (j c)", q=P, j=PACK)
+    pooled_rows = pooled.rearrange("n b k -> (n b) k")
+    p_rows = p.rearrange("n b t c -> (n b) (t c)")
+    out_rows = out.rearrange("n b c -> (n b) c")
+
+    with ExitStack() as ctx:
+        keep = ctx.enter_context(tc.tile_pool(name="keep", bufs=1))
+        landing = ctx.enter_context(tc.tile_pool(name="landing", bufs=6))
+        regrouped = ctx.enter_context(tc.tile_pool(name="regrouped", bufs=3))
+        quantised = ctx.enter_context(tc.tile_pool(name="quantised", bufs=3))
+        finish = ctx.enter_context(tc.tile_pool(name="finish", bufs=2))
+        psum_y = ctx.enter_context(tc.psum_pool(name="psum_y", bufs=1))
+        psum_t = ctx.enter_context(tc.psum_pool(name="psum_t", bufs=4))
+
+        ident = keep.tile([P, P], F32)
+        make_identity(nc, ident[:])
+
+        pooled_raw = landing.tile([P, ROW], BF16, tag="landing")
+        nc.sync.dma_start(out=pooled_raw[:], in_=pooled_rows)
+        p_raw = landing.tile([P, ROW], BF16, tag="landing")
+        nc.sync.dma_start(out=p_raw[:], in_=p_rows)
+
+        pooled_words = pooled_raw[:].bitcast(F32).rearrange("b (g q u) -> b g u q", q=P, u=2)
+        pooled_grouped = regrouped.tile([P, ROW], BF16, tag="grouped", align_bytes=64)
+        grouped_words = pooled_grouped[:].bitcast(F32).rearrange("q (g b u) -> q g b u", b=P, u=2)
+        pooled_codes = keep.tile([P, PASSES * P], U32, align_bytes=64)
+        pooled_scales = keep.tile([P, PASSES * P], U8, align_bytes=64)
+        for first in range(0, PASSES, 2):
+            turned = psum_t.tile([P, 2, 2, P], F32)
+            for g in range(2):
+                for u in range(2):
+                    nc.tensor.transpose(turned[:, g, u, :], pooled_words[:, first + g, u, :], ident[:])
+            copy = nc.scalar.copy if first % 4 == 0 else nc.vector.tensor_copy
+            copy(
+                out=grouped_words[:, first : first + 2],
+                in_=turned[:].rearrange("q g u b -> q g b u"),
+            )
+        for start in range(0, PASSES * P, HALF):
+            quantise(nc, pooled_grouped, pooled_codes, pooled_scales, start)
+
+        p_pairs = keep.tile([P, 2 * C], BF16)
+        nc.vector.tensor_max(out=p_pairs[:], in0=p_raw[:, : 2 * C], in1=p_raw[:, 2 * C :])
+        p_max = keep.tile([P, C], BF16)
+        nc.vector.tensor_max(out=p_max[:], in0=p_pairs[:, :C], in1=p_pairs[:, C:])
+
+        y = [psum_y.tile([P, BANK], F32, name="y%d" % bank) for bank in range(BANKS)]
+        lower = slice(0, HALF)
+        upper = slice(HALF, C)
+
+        def multiply(g, codes, scales, banks):
+            for bank in banks:
+                cols = slice(bank * BANK, (bank + 1) * BANK)
+                nc.tensor.matmul_mx(
+                    out=y[bank][:],
+                    lhsT=pooled_codes[:, g * P : (g + 1) * P].bitcast(FP8X4),
+                    lhsT_scale=pooled_scales[:, g * P : (g + 1) * P],
+                    rhs=codes[:, cols].bitcast(FP8X4),
+                    rhs_scale=scales[:, cols],
+                    start=(g == 0),
+                    stop=(g == PASSES - 1),
+                )
+
+        late = None
+        for g in range(PASSES):
+            raw = landing.tile([P, ROW], BF16, tag="landing")
+            nc.sync.dma_start(out=raw[:], in_=w_passes[g])
+            grouped = regrouped.tile([P, ROW], BF16, tag="grouped", align_bytes=64)
+            codes = quantised.tile([P, C], U32, align_bytes=64)
+            scales = quantised.tile([P, C], U8, align_bytes=64)
+            regroup(nc.vector.tensor_copy, raw, grouped, lower)
+            regroup(nc.scalar.copy, raw, grouped, upper)
+            if late is not None:
+                quantise(nc, late[1], late[2], late[3], HALF)
+                multiply(late[0], late[2], late[3], range(BANKS // 2, BANKS))
+            quantise(nc, grouped, codes, scales, 0)
+            multiply(g, codes, scales, range(BANKS // 2))
+            late = (g, grouped, codes, scales)
+        quantise(nc, late[1], late[2], late[3], HALF)
+        multiply(late[0], late[2], late[3], range(BANKS // 2, BANKS))
+
+        for bank in range(BANKS):
+            cols = slice(bank * BANK, (bank + 1) * BANK)
+            damped = finish.tile([P, BANK], F32)
+            nc.scalar.mul(out=damped[:], in_=y[bank][:], mul=LEAKY_SLOPE)
+            leaky = finish.tile([P, BANK], F32)
+            nc.vector.tensor_max(out=leaky[:], in0=y[bank][:], in1=damped[:])
+            feat = finish.tile([P, BANK], F32)
+            nc.vector.tensor_add(out=feat[:], in0=leaky[:], in1=p_max[:, cols])
+            nc.sync.dma_start(out=out_rows[:, cols], in_=feat[:])

@@ -14,32 +14,33 @@ PACK = 4
 K_PASS = P * PACK
 K = 8192
 C = 2048
-FRAMES = 4
 PASSES = K // K_PASS
 BANK = 512
-BANKS = C // BANK
 HALF = C // 2
 RUN = 4
 ROW = PACK * C
 LEAKY_SLOPE = 0.01
+VECTOR_PARTS = 15
+PARTS = 32
+P_BEFORE_PASS = 12
 
 FLOPS = 2 * P * K * C
 
 
-def regroup(copy, raw, grouped, cols):
-    src = raw.rearrange("q (j c) -> q j c", j=PACK)[:, :, cols]
-    dst = grouped.rearrange("q (c j) -> q c j", j=PACK)[:, cols, :]
+def regroup(copy, raw, grouped, first, stop):
+    src = raw.rearrange("q (j c) -> q j c", j=PACK)[:, :, first:stop]
+    dst = grouped.rearrange("q (c j) -> q c j", j=PACK)[:, first:stop, :]
     copy(
         out=dst.rearrange("q (n i) j -> q n j i", i=RUN),
         in_=src.rearrange("q j (n i) -> q n j i", i=RUN),
     )
 
 
-def quantise(nc, grouped, codes, scales, first):
+def quantise(nc, grouped, codes, scales, first, width):
     nc.vector.quantize_mx(
-        out=codes[:, first : first + HALF].bitcast(FP8X4),
-        scales=scales[:, first : first + HALF],
-        in_=grouped[:, PACK * first : PACK * (first + HALF)],
+        out=codes[:, first : first + width].bitcast(FP8X4),
+        scales=scales[:, first : first + width],
+        in_=grouped[:, PACK * first : PACK * (first + width)],
     )
 
 
@@ -64,9 +65,6 @@ def tile_gmpahead_pa_k_kernel(tc, pooled, p, Wout, out):
 
         pooled_raw = landing.tile([P, ROW], BF16, tag="landing")
         nc.sync.dma_start(out=pooled_raw[:], in_=pooled_rows)
-        p_raw = landing.tile([P, ROW], BF16, tag="landing")
-        nc.sync.dma_start(out=p_raw[:], in_=p_rows)
-
         pooled_words = pooled_raw[:].bitcast(F32).rearrange("b (g q u) -> b g u q", q=P, u=2)
         pooled_grouped = regrouped.tile([P, ROW], BF16, tag="grouped", align_bytes=64)
         grouped_words = pooled_grouped[:].bitcast(F32).rearrange("q (g b u) -> q g b u", b=P, u=2)
@@ -82,55 +80,63 @@ def tile_gmpahead_pa_k_kernel(tc, pooled, p, Wout, out):
                 out=grouped_words[:, first : first + 2],
                 in_=turned[:].rearrange("q g u b -> q g b u"),
             )
-        for start in range(0, PASSES * P, HALF):
-            quantise(nc, pooled_grouped, pooled_codes, pooled_scales, start)
+        for first in range(0, PASSES * P, HALF):
+            quantise(nc, pooled_grouped, pooled_codes, pooled_scales, first, HALF)
 
-        p_pairs = keep.tile([P, 2 * C], BF16)
-        nc.vector.tensor_max(out=p_pairs[:], in0=p_raw[:, : 2 * C], in1=p_raw[:, 2 * C :])
+        units = []
+        for g in range(PASSES):
+            width = BANK if g == PASSES - 1 else HALF
+            units.extend([(g, first, width) for first in range(0, C, width)])
+        y = [psum_y.tile([P, BANK], F32, name="y%d" % bank) for bank in range(C // BANK)]
         p_max = keep.tile([P, C], BF16)
-        nc.vector.tensor_max(out=p_max[:], in0=p_pairs[:, :C], in1=p_pairs[:, C:])
+        tiles = {}
 
-        y = [psum_y.tile([P, BANK], F32, name="y%d" % bank) for bank in range(BANKS)]
-        lower = slice(0, HALF)
-        upper = slice(HALF, C)
+        def load_and_regroup(g, first, width):
+            if first == 0:
+                if g == P_BEFORE_PASS:
+                    p_raw = landing.tile([P, ROW], BF16, tag="landing")
+                    nc.sync.dma_start(out=p_raw[:], in_=p_rows)
+                    p_pairs = keep.tile([P, 2 * C], BF16)
+                    nc.vector.tensor_max(out=p_pairs[:], in0=p_raw[:, : 2 * C], in1=p_raw[:, 2 * C :])
+                    nc.vector.tensor_max(out=p_max[:], in0=p_pairs[:, :C], in1=p_pairs[:, C:])
+                raw = landing.tile([P, ROW], BF16, tag="landing")
+                nc.sync.dma_start(out=raw[:], in_=w_passes[g])
+                grouped = regrouped.tile([P, ROW], BF16, tag="grouped", align_bytes=64)
+                codes = quantised.tile([P, C], U32, align_bytes=64)
+                scales = quantised.tile([P, C], U8, align_bytes=64)
+                tiles[g] = (raw, grouped, codes, scales)
+            raw, grouped = tiles[g][:2]
+            split = first + width * VECTOR_PARTS // PARTS
+            regroup(nc.vector.tensor_copy, raw, grouped, first, split)
+            regroup(nc.scalar.copy, raw, grouped, split, first + width)
 
-        def multiply(g, codes, scales, banks):
-            for bank in banks:
-                cols = slice(bank * BANK, (bank + 1) * BANK)
+        def quantise_and_multiply(g, first, width):
+            grouped, codes, scales = tiles[g][1:]
+            quantise(nc, grouped, codes, scales, first, width)
+            for start in range(first, first + width, BANK):
                 nc.tensor.matmul_mx(
-                    out=y[bank][:],
+                    out=y[start // BANK][:],
                     lhsT=pooled_codes[:, g * P : (g + 1) * P].bitcast(FP8X4),
                     lhsT_scale=pooled_scales[:, g * P : (g + 1) * P],
-                    rhs=codes[:, cols].bitcast(FP8X4),
-                    rhs_scale=scales[:, cols],
+                    rhs=codes[:, start : start + BANK].bitcast(FP8X4),
+                    rhs_scale=scales[:, start : start + BANK],
                     start=(g == 0),
                     stop=(g == PASSES - 1),
                 )
 
-        late = None
-        for g in range(PASSES):
-            raw = landing.tile([P, ROW], BF16, tag="landing")
-            nc.sync.dma_start(out=raw[:], in_=w_passes[g])
-            grouped = regrouped.tile([P, ROW], BF16, tag="grouped", align_bytes=64)
-            codes = quantised.tile([P, C], U32, align_bytes=64)
-            scales = quantised.tile([P, C], U8, align_bytes=64)
-            regroup(nc.vector.tensor_copy, raw, grouped, lower)
-            regroup(nc.scalar.copy, raw, grouped, upper)
-            if late is not None:
-                quantise(nc, late[1], late[2], late[3], HALF)
-                multiply(late[0], late[2], late[3], range(BANKS // 2, BANKS))
-            quantise(nc, grouped, codes, scales, 0)
-            multiply(g, codes, scales, range(BANKS // 2))
-            late = (g, grouped, codes, scales)
-        quantise(nc, late[1], late[2], late[3], HALF)
-        multiply(late[0], late[2], late[3], range(BANKS // 2, BANKS))
-
-        for bank in range(BANKS):
-            cols = slice(bank * BANK, (bank + 1) * BANK)
+        def finish_bank(first):
             damped = finish.tile([P, BANK], F32)
-            nc.scalar.mul(out=damped[:], in_=y[bank][:], mul=LEAKY_SLOPE)
+            nc.scalar.mul(out=damped[:], in_=y[first // BANK][:], mul=LEAKY_SLOPE)
             leaky = finish.tile([P, BANK], F32)
-            nc.vector.tensor_max(out=leaky[:], in0=y[bank][:], in1=damped[:])
+            nc.vector.tensor_max(out=leaky[:], in0=y[first // BANK][:], in1=damped[:])
             feat = finish.tile([P, BANK], F32)
-            nc.vector.tensor_add(out=feat[:], in0=leaky[:], in1=p_max[:, cols])
-            nc.sync.dma_start(out=out_rows[:, cols], in_=feat[:])
+            nc.vector.tensor_add(out=feat[:], in0=leaky[:], in1=p_max[:, first : first + BANK])
+            nc.sync.dma_start(out=out_rows[:, first : first + BANK], in_=feat[:])
+
+        for step in range(len(units) + 2):
+            if step < len(units):
+                load_and_regroup(*units[step])
+            if 1 <= step <= len(units):
+                quantise_and_multiply(*units[step - 1])
+            if step >= 2 and units[step - 2][0] == PASSES - 1:
+                finish_bank(units[step - 2][1])

@@ -17,7 +17,7 @@ C = 2048
 PASSES = K // K_PASS
 BANK = 512
 HALF = C // 2
-RUN = 4
+RUN = 8
 ROW = PACK * C
 LEAKY_SLOPE = 0.01
 VECTOR_PARTS = 15

@@ -22,14 +22,17 @@ ROW = PACK * C
 LEAKY_SLOPE = 0.01
 VECTOR_PARTS = 15
 PARTS = 32
-P_BEFORE_PASS = 12
+POOLED_PIECES = 4
+PIECE_PASSES = PASSES // POOLED_PIECES
+POOLED_BEHIND_PASS = [3, 4, 6, 8]
+P_BEHIND_PASS = [12, 13]
 
 FLOPS = 2 * P * K * C
 
 
-def regroup(copy, raw, grouped, first, stop):
-    src = raw.rearrange("q (j c) -> q j c", j=PACK)[:, :, first:stop]
-    dst = grouped.rearrange("q (c j) -> q c j", j=PACK)[:, first:stop, :]
+def regroup(copy, raw, base, grouped, first, stop):
+    src = raw.rearrange("q (j c) -> q j c", j=PACK)[:, :, first - base : stop - base]
+    dst = grouped[:].rearrange("q (c j) -> q c j", j=PACK)[:, first:stop, :]
     copy(
         out=dst.rearrange("q (n i) j -> q n j i", i=RUN),
         in_=src.rearrange("q j (n i) -> q n j i", i=RUN),
@@ -44,75 +47,79 @@ def quantise(nc, grouped, codes, scales, first, width):
     )
 
 
+def unit_width(g):
+    return {0: BANK, 1: HALF, PASSES - 2: HALF, PASSES - 1: BANK}.get(g, C)
+
+
 def tile_gmpahead_pa_k_kernel(tc, pooled, p, Wout, out):
     nc = tc.nc
-    w_passes = Wout.rearrange("n (g q j) c -> (n g) q (j c)", q=P, j=PACK)
+    w_passes = Wout.rearrange("n (g q j) c -> (n g) q j c", q=P, j=PACK)
     pooled_rows = pooled.rearrange("n b k -> (n b) k")
     p_rows = p.rearrange("n b t c -> (n b) (t c)")
     out_rows = out.rearrange("n b c -> (n b) c")
 
     with ExitStack() as ctx:
+        ctx.enter_context(tc.manual_schedule())
         keep = ctx.enter_context(tc.tile_pool(name="keep", bufs=1))
-        landing = ctx.enter_context(tc.tile_pool(name="landing", bufs=6))
+        landing = ctx.enter_context(tc.tile_pool(name="landing", bufs=4))
+        pieces = ctx.enter_context(tc.tile_pool(name="pieces", bufs=4))
+        halves = ctx.enter_context(tc.tile_pool(name="halves", bufs=2))
         regrouped = ctx.enter_context(tc.tile_pool(name="regrouped", bufs=3))
-        quantised = ctx.enter_context(tc.tile_pool(name="quantised", bufs=3))
+        pooled_regrouped = ctx.enter_context(tc.tile_pool(name="pooled_regrouped", bufs=1))
+        quantised = ctx.enter_context(tc.tile_pool(name="quantised", bufs=6))
         finish = ctx.enter_context(tc.tile_pool(name="finish", bufs=2))
         psum_y = ctx.enter_context(tc.psum_pool(name="psum_y", bufs=1))
         psum_t = ctx.enter_context(tc.psum_pool(name="psum_t", bufs=4))
 
+        warm = keep.tile([P, 2], F32)
+        nc.vector.memset(warm[:, 0:1], 0.0)
+        nc.scalar.mul(out=warm[:, 1:2], in_=warm[:, 0:1], mul=LEAKY_SLOPE)
         ident = keep.tile([P, P], F32)
         make_identity(nc, ident[:])
 
-        pooled_raw = landing.tile([P, ROW], BF16, tag="landing")
-        nc.sync.dma_start(out=pooled_raw[:], in_=pooled_rows)
-        pooled_words = pooled_raw[:].bitcast(F32).rearrange("b (g q u) -> b g u q", q=P, u=2)
-        pooled_grouped = regrouped.tile([P, ROW], BF16, tag="grouped", align_bytes=64)
-        grouped_words = pooled_grouped[:].bitcast(F32).rearrange("q (g b u) -> q g b u", b=P, u=2)
-        pooled_codes = keep.tile([P, PASSES * P], U32, align_bytes=64)
-        pooled_scales = keep.tile([P, PASSES * P], U8, align_bytes=64)
-        for first in range(0, PASSES, 2):
-            turned = psum_t.tile([P, 2, 2, P], F32)
-            for g in range(2):
-                for u in range(2):
-                    nc.tensor.transpose(turned[:, g, u, :], pooled_words[:, first + g, u, :], ident[:])
-            copy = nc.scalar.copy if first % 4 == 0 else nc.vector.tensor_copy
-            copy(
-                out=grouped_words[:, first : first + 2],
-                in_=turned[:].rearrange("q g u b -> q g b u"),
-            )
-        for first in range(0, PASSES * P, HALF):
-            quantise(nc, pooled_grouped, pooled_codes, pooled_scales, first, HALF)
-
-        units = []
-        for g in range(PASSES):
-            width = BANK if g == PASSES - 1 else HALF
-            units.extend([(g, first, width) for first in range(0, C, width)])
         y = [psum_y.tile([P, BANK], F32, name="y%d" % bank) for bank in range(C // BANK)]
         p_max = keep.tile([P, C], BF16)
+        p_pair = keep.tile([P, C], BF16)
+        pooled_codes = keep.tile([P, PASSES * P], U32, align_bytes=64)
+        pooled_scales = keep.tile([P, PASSES * P], U8, align_bytes=64)
+        sources = {}
         tiles = {}
 
-        def load_and_regroup(g, first, width):
-            if first == 0:
-                if g == P_BEFORE_PASS:
-                    p_raw = landing.tile([P, ROW], BF16, tag="landing")
-                    nc.sync.dma_start(out=p_raw[:], in_=p_rows)
-                    p_pairs = keep.tile([P, 2 * C], BF16)
-                    nc.vector.tensor_max(out=p_pairs[:], in0=p_raw[:, : 2 * C], in1=p_raw[:, 2 * C :])
-                    nc.vector.tensor_max(out=p_max[:], in0=p_pairs[:, :C], in1=p_pairs[:, C:])
+        def load(g):
+            if g in (0, 1):
+                width = unit_width(g)
+                pool, tag = {BANK: (pieces, "piece"), HALF: (halves, "half")}[width]
+                for first in range(0, C, width):
+                    part = pool.tile([P, PACK * width], BF16, tag=tag)
+                    nc.sync.dma_start(
+                        out=part[:].rearrange("q (j c) -> q j c", j=PACK),
+                        in_=w_passes[g][:, :, first : first + width],
+                    )
+                    sources[(g, first)] = (part[:], first)
+            else:
                 raw = landing.tile([P, ROW], BF16, tag="landing")
-                nc.sync.dma_start(out=raw[:], in_=w_passes[g])
-                grouped = regrouped.tile([P, ROW], BF16, tag="grouped", align_bytes=64)
-                codes = quantised.tile([P, C], U32, align_bytes=64)
-                scales = quantised.tile([P, C], U8, align_bytes=64)
-                tiles[g] = (raw, grouped, codes, scales)
-            raw, grouped = tiles[g][:2]
-            split = first + width * VECTOR_PARTS // PARTS
-            regroup(nc.vector.tensor_copy, raw, grouped, first, split)
-            regroup(nc.scalar.copy, raw, grouped, split, first + width)
+                nc.sync.dma_start(out=raw[:].rearrange("q (j c) -> q j c", j=PACK), in_=w_passes[g])
+                for first in range(0, C, unit_width(g)):
+                    sources[(g, first)] = (raw[:], 0)
 
-        def quantise_and_multiply(g, first, width):
-            grouped, codes, scales = tiles[g][1:]
-            quantise(nc, grouped, codes, scales, first, width)
+        def prepare(g):
+            grouped = regrouped.tile([P, ROW], BF16, tag="grouped", align_bytes=64)
+            codes = quantised.tile([P, C], U32, align_bytes=64)
+            scales = quantised.tile([P, C], U8, align_bytes=64)
+            tiles[g] = (grouped, codes, scales)
+
+        def regroup_unit(g, first, width):
+            raw, base = sources[(g, first)]
+            split = first + width * VECTOR_PARTS // PARTS
+            regroup(nc.vector.tensor_copy, raw, base, tiles[g][0], first, split)
+            regroup(nc.scalar.copy, raw, base, tiles[g][0], split, first + width)
+
+        def quantise_unit(g, first, width):
+            for start in range(first, first + width, HALF):
+                quantise(nc, *tiles[g], start, min(width, HALF))
+
+        def multiply_unit(g, first, width):
+            codes, scales = tiles[g][1:]
             for start in range(first, first + width, BANK):
                 nc.tensor.matmul_mx(
                     out=y[start // BANK][:],
@@ -133,10 +140,99 @@ def tile_gmpahead_pa_k_kernel(tc, pooled, p, Wout, out):
             nc.vector.tensor_add(out=feat[:], in0=leaky[:], in1=p_max[:, first : first + BANK])
             nc.sync.dma_start(out=out_rows[:, first : first + BANK], in_=feat[:])
 
-        for step in range(len(units) + 2):
-            if step < len(units):
-                load_and_regroup(*units[step])
-            if 1 <= step <= len(units):
-                quantise_and_multiply(*units[step - 1])
-            if step >= 2 and units[step - 2][0] == PASSES - 1:
-                finish_bank(units[step - 2][1])
+        def load_pooled(i):
+            part = pieces.tile([P, PIECE_PASSES * K_PASS], BF16, tag="piece")
+            first = i * PIECE_PASSES * K_PASS
+            nc.sync.dma_start(out=part[:], in_=pooled_rows[:, first : first + PIECE_PASSES * K_PASS])
+            sources[("pooled", i)] = part
+
+        def turn_pooled(i):
+            words = sources[("pooled", i)][:].bitcast(F32).rearrange("b (g q u) -> b g u q", q=P, u=2)
+            banks = []
+            for first in range(0, PIECE_PASSES, 2):
+                turned = psum_t.tile([P, 2, 2, P], F32)
+                for g in range(2):
+                    for u in range(2):
+                        nc.tensor.transpose(turned[:, g, u, :], words[:, first + g, u, :], ident[:])
+                banks.append(turned)
+            sources[("turned", i)] = banks
+
+        def regroup_pooled(i):
+            grouped = pooled_regrouped.tile([P, PIECE_PASSES * P * PACK], BF16, align_bytes=64)
+            words = grouped[:].bitcast(F32).rearrange("q (g b u) -> q g b u", b=P, u=2)
+            for bank, copy in enumerate([nc.scalar.copy, nc.vector.tensor_copy]):
+                copy(
+                    out=words[:, 2 * bank : 2 * bank + 2],
+                    in_=sources[("turned", i)][bank][:].rearrange("q g u b -> q g b u"),
+                )
+            tiles[("pooled", i)] = grouped
+
+        def quantise_pooled(i):
+            first = i * PIECE_PASSES * P
+            nc.vector.quantize_mx(
+                out=pooled_codes[:, first : first + PIECE_PASSES * P].bitcast(FP8X4),
+                scales=pooled_scales[:, first : first + PIECE_PASSES * P],
+                in_=tiles[("pooled", i)][:],
+            )
+
+        def load_p(i):
+            part = halves.tile([P, 2 * C], BF16, tag="half")
+            nc.sync.dma_start(out=part[:], in_=p_rows[:, 2 * C * i : 2 * C * (i + 1)])
+            sources[("p", i)] = part
+
+        def reduce_p(i):
+            part = sources[("p", i)]
+            best = p_max if i == 0 else p_pair
+            nc.vector.tensor_max(out=best[:], in0=part[:, :C], in1=part[:, C:])
+
+        steps = []
+        for g in range(PASSES):
+            steps.extend([("w", g, first, unit_width(g)) for first in range(0, C, unit_width(g))])
+            if g in POOLED_BEHIND_PASS:
+                steps.append(("pooled", POOLED_BEHIND_PASS.index(g)))
+            if g in P_BEHIND_PASS:
+                steps.append(("p", P_BEHIND_PASS.index(g)))
+
+        def load_step(kind, *which):
+            if kind == "w":
+                if which[1] == 0:
+                    load(which[0])
+                    prepare(which[0])
+            elif kind == "pooled":
+                load_pooled(*which)
+                turn_pooled(*which)
+            else:
+                load_p(*which)
+
+        def regroup_step(kind, *which):
+            if kind == "w":
+                regroup_unit(*which)
+            elif kind == "pooled":
+                regroup_pooled(*which)
+            else:
+                reduce_p(*which)
+
+        waiting = []
+        pooled_pieces = 0
+        load_step(*steps[0])
+        for step in range(len(steps) + 2):
+            if step + 1 < len(steps):
+                load_step(*steps[step + 1])
+            if step < len(steps):
+                regroup_step(*steps[step])
+            if 1 <= step <= len(steps):
+                kind, *which = steps[step - 1]
+                if kind == "w":
+                    quantise_unit(*which)
+                    waiting.append(which)
+                elif kind == "pooled":
+                    quantise_pooled(*which)
+                    pooled_pieces = which[0] + 1
+                elif which[0] == 1:
+                    nc.vector.tensor_max(out=p_max[:], in0=p_max[:], in1=p_pair[:])
+                ready = [unit for unit in waiting if unit[0] < pooled_pieces * PIECE_PASSES]
+                waiting = [unit for unit in waiting if unit not in ready]
+                for unit in ready:
+                    multiply_unit(*unit)
+            if step >= 2 and steps[step - 2][:2] == ("w", PASSES - 1):
+                finish_bank(steps[step - 2][2])

@@ -9,6 +9,7 @@ U32 = mybir.dt.uint32
 U8 = mybir.dt.uint8
 FP8X4 = mybir.dt.float8_e4m3fn_x4
 
+FRAMES = 4
 P = 128
 PACK = 4
 K_PASS = P * PACK
@@ -20,18 +21,18 @@ HALF = C // 2
 RUN = 8
 ROW = PACK * C
 LEAKY_SLOPE = 0.01
-VECTOR_PARTS = 15
-PARTS = 32
+VECTOR_PARTS = 1
+PARTS = 2
+MULTIPLIED_AT_ONCE = 2
 POOLED_PIECES = 4
 PIECE_PASSES = PASSES // POOLED_PIECES
-POOLED_BEHIND_PASS = [3, 4, 6, 8]
-P_BEHIND_PASS = [12, 13]
+POOLED_BEHIND_PASS = [2, 4, 8, 12]
 
 FLOPS = 2 * P * K * C
 
 
-def regroup(copy, raw, base, grouped, first, stop):
-    src = raw.rearrange("q (j c) -> q j c", j=PACK)[:, :, first - base : stop - base]
+def regroup(copy, raw, grouped, first, stop):
+    src = raw[:].rearrange("q (j c) -> q j c", j=PACK)[:, :, first:stop]
     dst = grouped[:].rearrange("q (c j) -> q c j", j=PACK)[:, first:stop, :]
     copy(
         out=dst.rearrange("q (n i) j -> q n j i", i=RUN),
@@ -47,26 +48,21 @@ def quantise(nc, grouped, codes, scales, first, width):
     )
 
 
-def unit_width(g):
-    return {0: BANK, 1: HALF, PASSES - 2: HALF, PASSES - 1: BANK}.get(g, C)
-
-
 def tile_gmpahead_pa_k_kernel(tc, pooled, p, Wout, out):
     nc = tc.nc
-    w_passes = Wout.rearrange("n (g q j) c -> (n g) q j c", q=P, j=PACK)
+    w_passes = Wout.rearrange("n (g q j) c -> (n g) q (j c)", q=P, j=PACK)
     pooled_rows = pooled.rearrange("n b k -> (n b) k")
-    p_rows = p.rearrange("n b t c -> (n b) (t c)")
+    p_rows = p.rearrange("n b t c -> (n b) t c")
     out_rows = out.rearrange("n b c -> (n b) c")
 
     with ExitStack() as ctx:
         ctx.enter_context(tc.manual_schedule())
         keep = ctx.enter_context(tc.tile_pool(name="keep", bufs=1))
-        landing = ctx.enter_context(tc.tile_pool(name="landing", bufs=4))
-        pieces = ctx.enter_context(tc.tile_pool(name="pieces", bufs=4))
-        halves = ctx.enter_context(tc.tile_pool(name="halves", bufs=2))
+        landing = ctx.enter_context(tc.tile_pool(name="landing", bufs=6))
+        pieces = ctx.enter_context(tc.tile_pool(name="pieces", bufs=2))
         regrouped = ctx.enter_context(tc.tile_pool(name="regrouped", bufs=3))
         pooled_regrouped = ctx.enter_context(tc.tile_pool(name="pooled_regrouped", bufs=1))
-        quantised = ctx.enter_context(tc.tile_pool(name="quantised", bufs=6))
+        quantised = ctx.enter_context(tc.tile_pool(name="quantised", bufs=4))
         finish = ctx.enter_context(tc.tile_pool(name="finish", bufs=2))
         psum_y = ctx.enter_context(tc.psum_pool(name="psum_y", bufs=1))
         psum_t = ctx.enter_context(tc.psum_pool(name="psum_t", bufs=4))
@@ -79,28 +75,15 @@ def tile_gmpahead_pa_k_kernel(tc, pooled, p, Wout, out):
 
         y = [psum_y.tile([P, BANK], F32, name="y%d" % bank) for bank in range(C // BANK)]
         p_max = keep.tile([P, C], BF16)
-        p_pair = keep.tile([P, C], BF16)
         pooled_codes = keep.tile([P, PASSES * P], U32, align_bytes=64)
         pooled_scales = keep.tile([P, PASSES * P], U8, align_bytes=64)
         sources = {}
         tiles = {}
 
         def load(g):
-            if g in (0, 1):
-                width = unit_width(g)
-                pool, tag = {BANK: (pieces, "piece"), HALF: (halves, "half")}[width]
-                for first in range(0, C, width):
-                    part = pool.tile([P, PACK * width], BF16, tag=tag)
-                    nc.sync.dma_start(
-                        out=part[:].rearrange("q (j c) -> q j c", j=PACK),
-                        in_=w_passes[g][:, :, first : first + width],
-                    )
-                    sources[(g, first)] = (part[:], first)
-            else:
-                raw = landing.tile([P, ROW], BF16, tag="landing")
-                nc.sync.dma_start(out=raw[:].rearrange("q (j c) -> q j c", j=PACK), in_=w_passes[g])
-                for first in range(0, C, unit_width(g)):
-                    sources[(g, first)] = (raw[:], 0)
+            raw = landing.tile([P, ROW], BF16, tag="landing")
+            nc.sync.dma_start(out=raw[:], in_=w_passes[g])
+            sources[g] = raw
 
         def prepare(g):
             grouped = regrouped.tile([P, ROW], BF16, tag="grouped", align_bytes=64)
@@ -109,14 +92,12 @@ def tile_gmpahead_pa_k_kernel(tc, pooled, p, Wout, out):
             tiles[g] = (grouped, codes, scales)
 
         def regroup_unit(g, first, width):
-            raw, base = sources[(g, first)]
             split = first + width * VECTOR_PARTS // PARTS
-            regroup(nc.vector.tensor_copy, raw, base, tiles[g][0], first, split)
-            regroup(nc.scalar.copy, raw, base, tiles[g][0], split, first + width)
+            regroup(nc.vector.tensor_copy, sources[g], tiles[g][0], first, split)
+            regroup(nc.scalar.copy, sources[g], tiles[g][0], split, first + width)
 
         def quantise_unit(g, first, width):
-            for start in range(first, first + width, HALF):
-                quantise(nc, *tiles[g], start, min(width, HALF))
+            quantise(nc, *tiles[g], first, width)
 
         def multiply_unit(g, first, width):
             codes, scales = tiles[g][1:]
@@ -160,8 +141,8 @@ def tile_gmpahead_pa_k_kernel(tc, pooled, p, Wout, out):
         def regroup_pooled(i):
             grouped = pooled_regrouped.tile([P, PIECE_PASSES * P * PACK], BF16, align_bytes=64)
             words = grouped[:].bitcast(F32).rearrange("q (g b u) -> q g b u", b=P, u=2)
-            for bank, copy in enumerate([nc.scalar.copy, nc.vector.tensor_copy]):
-                copy(
+            for bank in range(2):
+                nc.scalar.copy(
                     out=words[:, 2 * bank : 2 * bank + 2],
                     in_=sources[("turned", i)][bank][:].rearrange("q g u b -> q g b u"),
                 )
@@ -175,23 +156,27 @@ def tile_gmpahead_pa_k_kernel(tc, pooled, p, Wout, out):
                 in_=tiles[("pooled", i)][:],
             )
 
-        def load_p(i):
-            part = halves.tile([P, 2 * C], BF16, tag="half")
-            nc.sync.dma_start(out=part[:], in_=p_rows[:, 2 * C * i : 2 * C * (i + 1)])
-            sources[("p", i)] = part
+        def load_p(first):
+            part = landing.tile([P, FRAMES, HALF], BF16, tag="landing")
+            nc.sync.dma_start(out=part[:], in_=p_rows[:, :, first : first + HALF])
+            sources[("p", first)] = part
 
-        def reduce_p(i):
-            part = sources[("p", i)]
-            best = p_max if i == 0 else p_pair
-            nc.vector.tensor_max(out=best[:], in0=part[:, :C], in1=part[:, C:])
+        def reduce_p(first):
+            part = sources[("p", first)]
+            pairs = finish.tile([P, 2, HALF], BF16)
+            nc.vector.tensor_max(out=pairs[:], in0=part[:, :2], in1=part[:, 2:])
+            tiles[("p", first)] = pairs
+
+        def reduce_pairs(first):
+            pairs = tiles[("p", first)]
+            nc.vector.tensor_max(out=p_max[:, first : first + HALF], in0=pairs[:, 0], in1=pairs[:, 1])
 
         steps = []
         for g in range(PASSES):
-            steps.extend([("w", g, first, unit_width(g)) for first in range(0, C, unit_width(g))])
+            steps.extend([("w", g, first, HALF) for first in range(0, C, HALF)])
             if g in POOLED_BEHIND_PASS:
                 steps.append(("pooled", POOLED_BEHIND_PASS.index(g)))
-            if g in P_BEHIND_PASS:
-                steps.append(("p", P_BEHIND_PASS.index(g)))
+        steps.append(("p", 0))
 
         def load_step(kind, *which):
             if kind == "w":
@@ -202,7 +187,8 @@ def tile_gmpahead_pa_k_kernel(tc, pooled, p, Wout, out):
                 load_pooled(*which)
                 turn_pooled(*which)
             else:
-                load_p(*which)
+                for first in range(0, C, HALF):
+                    load_p(first)
 
         def regroup_step(kind, *which):
             if kind == "w":
@@ -215,24 +201,27 @@ def tile_gmpahead_pa_k_kernel(tc, pooled, p, Wout, out):
         waiting = []
         pooled_pieces = 0
         load_step(*steps[0])
-        for step in range(len(steps) + 2):
+        for step in range(len(steps)):
             if step + 1 < len(steps):
                 load_step(*steps[step + 1])
-            if step < len(steps):
-                regroup_step(*steps[step])
-            if 1 <= step <= len(steps):
+            regroup_step(*steps[step])
+            if step >= 1:
                 kind, *which = steps[step - 1]
                 if kind == "w":
                     quantise_unit(*which)
                     waiting.append(which)
-                elif kind == "pooled":
+                else:
                     quantise_pooled(*which)
                     pooled_pieces = which[0] + 1
-                elif which[0] == 1:
-                    nc.vector.tensor_max(out=p_max[:], in0=p_max[:], in1=p_pair[:])
                 ready = [unit for unit in waiting if unit[0] < pooled_pieces * PIECE_PASSES]
-                waiting = [unit for unit in waiting if unit not in ready]
+                ready = ready[:MULTIPLIED_AT_ONCE]
+                waiting = waiting[len(ready) :]
                 for unit in ready:
                     multiply_unit(*unit)
-            if step >= 2 and steps[step - 2][:2] == ("w", PASSES - 1):
-                finish_bank(steps[step - 2][2])
+        reduce_pairs(0)
+        finish_bank(0)
+        reduce_p(HALF)
+        finish_bank(BANK)
+        reduce_pairs(HALF)
+        finish_bank(HALF)
+        finish_bank(HALF + BANK)

@@ -21,8 +21,8 @@ HALF = C // 2
 RUN = 8
 ROW = PACK * C
 LEAKY_SLOPE = 0.01
-VECTOR_PARTS = 1
-PARTS = 2
+TENSOR_COLUMNS = 96
+VECTOR_COLUMNS = 480
 MULTIPLIED_AT_ONCE = 2
 POOLED_PIECES = 4
 PIECE_PASSES = PASSES // POOLED_PIECES
@@ -72,12 +72,15 @@ def tile_gmpahead_pa_k_kernel(tc, pooled, p, Wout, out):
         nc.scalar.mul(out=warm[:, 1:2], in_=warm[:, 0:1], mul=LEAKY_SLOPE)
         ident = keep.tile([P, P], F32)
         make_identity(nc, ident[:])
+        ident_bf16 = keep.tile([P, P], BF16)
+        make_identity(nc, ident_bf16[:])
 
         y = [psum_y.tile([P, BANK], F32, name="y%d" % bank) for bank in range(C // BANK)]
         p_max = keep.tile([P, C], BF16)
         pooled_codes = keep.tile([P, PASSES * P], U32, align_bytes=64)
         pooled_scales = keep.tile([P, PASSES * P], U8, align_bytes=64)
         sources = {}
+        moved = {}
         tiles = {}
 
         def load(g):
@@ -92,9 +95,25 @@ def tile_gmpahead_pa_k_kernel(tc, pooled, p, Wout, out):
             tiles[g] = (grouped, codes, scales)
 
         def regroup_unit(g, first, width):
-            split = first + width * VECTOR_PARTS // PARTS
-            regroup(nc.vector.tensor_copy, sources[g], tiles[g][0], first, split)
-            regroup(nc.scalar.copy, sources[g], tiles[g][0], split, first + width)
+            split = first + VECTOR_COLUMNS
+            stop = first + width - TENSOR_COLUMNS
+            grouped = tiles[g][0]
+            regroup(nc.vector.tensor_copy, sources[g], grouped, first, split)
+            regroup(nc.scalar.copy, sources[g], grouped, split, stop)
+            nc.scalar.copy(out=grouped[:, PACK * stop : PACK * (first + width)], in_=moved[(g, first)][:])
+
+        def regroup_on_tensor(g, first, width):
+            product = psum_t.tile([P, TENSOR_COLUMNS * PACK], BF16, tag="transit")
+            stop = first + width
+            rows = sources[g][:].rearrange("q (j c) -> q j c", j=PACK)
+            nc.tensor.matmul(
+                product[:].rearrange("q (c j) -> q j c", j=PACK),
+                lhsT=ident_bf16[:],
+                rhs=rows[:, :, stop - TENSOR_COLUMNS : stop],
+                start=True,
+                stop=True,
+            )
+            moved[(g, first)] = product
 
         def quantise_unit(g, first, width):
             quantise(nc, *tiles[g], first, width)
@@ -131,7 +150,7 @@ def tile_gmpahead_pa_k_kernel(tc, pooled, p, Wout, out):
             words = sources[("pooled", i)][:].bitcast(F32).rearrange("b (g q u) -> b g u q", q=P, u=2)
             banks = []
             for first in range(0, PIECE_PASSES, 2):
-                turned = psum_t.tile([P, 2, 2, P], F32)
+                turned = psum_t.tile([P, 2, 2, P], F32, tag="transit")
                 for g in range(2):
                     for u in range(2):
                         nc.tensor.transpose(turned[:, g, u, :], words[:, first + g, u, :], ident[:])
@@ -183,6 +202,7 @@ def tile_gmpahead_pa_k_kernel(tc, pooled, p, Wout, out):
                 if which[1] == 0:
                     load(which[0])
                     prepare(which[0])
+                regroup_on_tensor(*which)
             elif kind == "pooled":
                 load_pooled(*which)
                 turn_pooled(*which)

@@ -52,7 +52,7 @@ def tile_gmpahead_pa_k_kernel(tc, pooled, p, Wout, out):
     nc = tc.nc
     w_passes = Wout.rearrange("n (g q j) c -> (n g) q (j c)", q=P, j=PACK)
     pooled_rows = pooled.rearrange("n b k -> (n b) k")
-    p_rows = p.rearrange("n b t c -> (n b) t c")
+    p_rows = p.rearrange("n b t c -> (n b) (t c)")
     out_rows = out.rearrange("n b c -> (n b) c")
 
     with ExitStack() as ctx:
@@ -79,6 +79,7 @@ def tile_gmpahead_pa_k_kernel(tc, pooled, p, Wout, out):
         p_max = keep.tile([P, C], BF16)
         pooled_codes = keep.tile([P, PASSES * P], U32, align_bytes=64)
         pooled_scales = keep.tile([P, PASSES * P], U8, align_bytes=64)
+        leaky = {}
         sources = {}
         moved = {}
         tiles = {}
@@ -131,14 +132,16 @@ def tile_gmpahead_pa_k_kernel(tc, pooled, p, Wout, out):
                     stop=(g == PASSES - 1),
                 )
 
-        def finish_bank(first):
+        def relu_bank(bank):
             damped = finish.tile([P, BANK], F32)
-            nc.scalar.mul(out=damped[:], in_=y[first // BANK][:], mul=LEAKY_SLOPE)
-            leaky = finish.tile([P, BANK], F32)
-            nc.vector.tensor_max(out=leaky[:], in0=y[first // BANK][:], in1=damped[:])
-            feat = finish.tile([P, BANK], F32)
-            nc.vector.tensor_add(out=feat[:], in0=leaky[:], in1=p_max[:, first : first + BANK])
-            nc.sync.dma_start(out=out_rows[:, first : first + BANK], in_=feat[:])
+            nc.scalar.mul(out=damped[:], in_=y[bank][:], mul=LEAKY_SLOPE)
+            leaky[bank] = keep.tile([P, BANK], F32, name="leaky%d" % bank)
+            nc.vector.tensor_max(out=leaky[bank][:], in0=y[bank][:], in1=damped[:])
+
+        def add_and_store(bank):
+            columns = slice(bank * BANK, (bank + 1) * BANK)
+            nc.vector.tensor_add(out=leaky[bank][:], in0=leaky[bank][:], in1=p_max[:, columns])
+            nc.sync.dma_start(out=out_rows[:, columns], in_=leaky[bank][:])
 
         def load_pooled(i):
             part = pieces.tile([P, PIECE_PASSES * K_PASS], BF16, tag="piece")
@@ -175,27 +178,23 @@ def tile_gmpahead_pa_k_kernel(tc, pooled, p, Wout, out):
                 in_=tiles[("pooled", i)][:],
             )
 
-        def load_p(first):
-            part = landing.tile([P, FRAMES, HALF], BF16, tag="landing")
-            nc.sync.dma_start(out=part[:], in_=p_rows[:, :, first : first + HALF])
-            sources[("p", first)] = part
+        def load_p():
+            for frames in [range(FRAMES - 1), range(FRAMES - 1, FRAMES)]:
+                part = landing.tile([P, len(frames) * C], BF16, tag="landing")
+                nc.sync.dma_start(out=part[:], in_=p_rows[:, C * frames.start : C * frames.stop])
+                for place, frame in enumerate(frames):
+                    sources[("p", frame)] = part[:, C * place : C * (place + 1)]
 
-        def reduce_p(first):
-            part = sources[("p", first)]
-            pairs = finish.tile([P, 2, HALF], BF16)
-            nc.vector.tensor_max(out=pairs[:], in0=part[:, :2], in1=part[:, 2:])
-            tiles[("p", first)] = pairs
-
-        def reduce_pairs(first):
-            pairs = tiles[("p", first)]
-            nc.vector.tensor_max(out=p_max[:, first : first + HALF], in0=pairs[:, 0], in1=pairs[:, 1])
+        def take_frame(frame):
+            best = sources[("p", 0)] if frame == 1 else p_max[:]
+            nc.vector.tensor_max(out=p_max[:], in0=best, in1=sources[("p", frame)])
 
         steps = []
         for g in range(PASSES):
             steps.extend([("w", g, first, HALF) for first in range(0, C, HALF)])
             if g in POOLED_BEHIND_PASS:
                 steps.append(("pooled", POOLED_BEHIND_PASS.index(g)))
-        steps.append(("p", 0))
+        steps.append(("p", 1))
 
         def load_step(kind, *which):
             if kind == "w":
@@ -207,8 +206,7 @@ def tile_gmpahead_pa_k_kernel(tc, pooled, p, Wout, out):
                 load_pooled(*which)
                 turn_pooled(*which)
             else:
-                for first in range(0, C, HALF):
-                    load_p(first)
+                load_p()
 
         def regroup_step(kind, *which):
             if kind == "w":
@@ -216,7 +214,7 @@ def tile_gmpahead_pa_k_kernel(tc, pooled, p, Wout, out):
             elif kind == "pooled":
                 regroup_pooled(*which)
             else:
-                reduce_p(*which)
+                take_frame(*which)
 
         waiting = []
         pooled_pieces = 0
@@ -238,10 +236,10 @@ def tile_gmpahead_pa_k_kernel(tc, pooled, p, Wout, out):
                 waiting = waiting[len(ready) :]
                 for unit in ready:
                     multiply_unit(*unit)
-        reduce_pairs(0)
-        finish_bank(0)
-        reduce_p(HALF)
-        finish_bank(BANK)
-        reduce_pairs(HALF)
-        finish_bank(HALF)
-        finish_bank(HALF + BANK)
+        take_frame(2)
+        for bank in range(3):
+            relu_bank(bank)
+        take_frame(3)
+        relu_bank(3)
+        for bank in range(4):
+            add_and_store(bank)

@@ -22,7 +22,7 @@ RUN = 8
 ROW = PACK * C
 LEAKY_SLOPE = 0.01
 TENSOR_COLUMNS = 96
-VECTOR_COLUMNS = 480
+VECTOR_COLUMNS = {HALF: 480, BANK: 96}
 MULTIPLIED_AT_ONCE = 2
 POOLED_PIECES = 4
 PIECE_PASSES = PASSES // POOLED_PIECES
@@ -96,7 +96,7 @@ def tile_gmpahead_pa_k_kernel(tc, pooled, p, Wout, out):
             tiles[g] = (grouped, codes, scales)
 
         def regroup_unit(g, first, width):
-            split = first + VECTOR_COLUMNS
+            split = first + VECTOR_COLUMNS[width]
             stop = first + width - TENSOR_COLUMNS
             grouped = tiles[g][0]
             regroup(nc.vector.tensor_copy, sources[g], grouped, first, split)
@@ -190,11 +190,10 @@ def tile_gmpahead_pa_k_kernel(tc, pooled, p, Wout, out):
             nc.vector.tensor_max(out=p_max[:], in0=best, in1=sources[("p", frame)])
 
         steps = []
-        for g in range(PASSES):
+        for g in range(PASSES - 1):
             steps.extend([("w", g, first, HALF) for first in range(0, C, HALF)])
             if g in POOLED_BEHIND_PASS:
                 steps.append(("pooled", POOLED_BEHIND_PASS.index(g)))
-        steps.append(("p", 1))
 
         def load_step(kind, *which):
             if kind == "w":
@@ -202,19 +201,15 @@ def tile_gmpahead_pa_k_kernel(tc, pooled, p, Wout, out):
                     load(which[0])
                     prepare(which[0])
                 regroup_on_tensor(*which)
-            elif kind == "pooled":
+            else:
                 load_pooled(*which)
                 turn_pooled(*which)
-            else:
-                load_p()
 
         def regroup_step(kind, *which):
             if kind == "w":
                 regroup_unit(*which)
-            elif kind == "pooled":
-                regroup_pooled(*which)
             else:
-                take_frame(*which)
+                regroup_pooled(*which)
 
         waiting = []
         pooled_pieces = 0
@@ -236,10 +231,24 @@ def tile_gmpahead_pa_k_kernel(tc, pooled, p, Wout, out):
                 waiting = waiting[len(ready) :]
                 for unit in ready:
                     multiply_unit(*unit)
-        take_frame(2)
-        for bank in range(3):
-            relu_bank(bank)
+        last_units = [(PASSES - 1, first, BANK) for first in range(0, C, BANK)]
+        load(PASSES - 1)
+        prepare(PASSES - 1)
+        load_p()
+        for unit in last_units:
+            regroup_on_tensor(*unit)
+        quantise_unit(*steps[-1][1:])
+        multiply_unit(*steps[-1][1:])
+        for unit in last_units:
+            regroup_unit(*unit)
+        for bank, unit in enumerate(last_units):
+            quantise_unit(*unit)
+            multiply_unit(*unit)
+            if bank in (1, 2):
+                take_frame(bank)
+        relu_bank(0)
         take_frame(3)
-        relu_bank(3)
-        for bank in range(4):
+        for bank in range(1, len(y)):
+            relu_bank(bank)
+        for bank in range(len(y)):
             add_and_store(bank)

@@ -9,7 +9,6 @@ U32 = mybir.dt.uint32
 U8 = mybir.dt.uint8
 FP8X4 = mybir.dt.float8_e4m3fn_x4
 
-FRAMES = 4
 P = 128
 PACK = 4
 K_PASS = P * PACK
@@ -21,12 +20,13 @@ HALF = C // 2
 RUN = 8
 ROW = PACK * C
 LEAKY_SLOPE = 0.01
-TENSOR_COLUMNS = 96
-VECTOR_COLUMNS = {HALF: 480, BANK: 96}
+TENSOR_COLUMNS = {HALF: 88, BANK: 128}
+VECTOR_COLUMNS = {HALF: 480, BANK: 64}
 MULTIPLIED_AT_ONCE = 2
 POOLED_PIECES = 4
 PIECE_PASSES = PASSES // POOLED_PIECES
-POOLED_BEHIND_PASS = [2, 4, 8, 12]
+POOLED_BEHIND_PASS = [2, 4, 8]
+FRAMES_OF_LOAD = [(0, 1), (2,), (3,)]
 
 FLOPS = 2 * P * K * C
 
@@ -58,12 +58,11 @@ def tile_gmpahead_pa_k_kernel(tc, pooled, p, Wout, out):
     with ExitStack() as ctx:
         ctx.enter_context(tc.manual_schedule())
         keep = ctx.enter_context(tc.tile_pool(name="keep", bufs=1))
-        landing = ctx.enter_context(tc.tile_pool(name="landing", bufs=6))
+        landing = ctx.enter_context(tc.tile_pool(name="landing", bufs=5))
         pieces = ctx.enter_context(tc.tile_pool(name="pieces", bufs=2))
         regrouped = ctx.enter_context(tc.tile_pool(name="regrouped", bufs=3))
         pooled_regrouped = ctx.enter_context(tc.tile_pool(name="pooled_regrouped", bufs=1))
-        quantised = ctx.enter_context(tc.tile_pool(name="quantised", bufs=4))
-        finish = ctx.enter_context(tc.tile_pool(name="finish", bufs=2))
+        quantised = ctx.enter_context(tc.tile_pool(name="quantised", bufs=5))
         psum_y = ctx.enter_context(tc.psum_pool(name="psum_y", bufs=1))
         psum_t = ctx.enter_context(tc.psum_pool(name="psum_t", bufs=4))
 
@@ -79,6 +78,7 @@ def tile_gmpahead_pa_k_kernel(tc, pooled, p, Wout, out):
         p_max = keep.tile([P, C], BF16)
         pooled_codes = keep.tile([P, PASSES * P], U32, align_bytes=64)
         pooled_scales = keep.tile([P, PASSES * P], U8, align_bytes=64)
+        damped = {}
         leaky = {}
         sources = {}
         moved = {}
@@ -95,22 +95,25 @@ def tile_gmpahead_pa_k_kernel(tc, pooled, p, Wout, out):
             scales = quantised.tile([P, C], U8, align_bytes=64)
             tiles[g] = (grouped, codes, scales)
 
-        def regroup_unit(g, first, width):
+        def regroup_on_vector(g, first, width):
+            regroup(nc.vector.tensor_copy, sources[g], tiles[g][0], first, first + VECTOR_COLUMNS[width])
+
+        def regroup_on_scalar(g, first, width):
             split = first + VECTOR_COLUMNS[width]
-            stop = first + width - TENSOR_COLUMNS
+            stop = first + width - TENSOR_COLUMNS[width]
             grouped = tiles[g][0]
-            regroup(nc.vector.tensor_copy, sources[g], grouped, first, split)
             regroup(nc.scalar.copy, sources[g], grouped, split, stop)
             nc.scalar.copy(out=grouped[:, PACK * stop : PACK * (first + width)], in_=moved[(g, first)][:])
 
         def regroup_on_tensor(g, first, width):
-            product = psum_t.tile([P, TENSOR_COLUMNS * PACK], BF16, tag="transit")
+            columns = TENSOR_COLUMNS[width]
+            product = psum_t.tile([P, columns * PACK], BF16, tag="transit")
             stop = first + width
             rows = sources[g][:].rearrange("q (j c) -> q j c", j=PACK)
             nc.tensor.matmul(
                 product[:].rearrange("q (c j) -> q j c", j=PACK),
                 lhsT=ident_bf16[:],
-                rhs=rows[:, :, stop - TENSOR_COLUMNS : stop],
+                rhs=rows[:, :, stop - columns : stop],
                 start=True,
                 stop=True,
             )
@@ -132,15 +135,17 @@ def tile_gmpahead_pa_k_kernel(tc, pooled, p, Wout, out):
                     stop=(g == PASSES - 1),
                 )
 
-        def relu_bank(bank):
-            damped = finish.tile([P, BANK], F32)
-            nc.scalar.mul(out=damped[:], in_=y[bank][:], mul=LEAKY_SLOPE)
-            leaky[bank] = keep.tile([P, BANK], F32, name="leaky%d" % bank)
-            nc.vector.tensor_max(out=leaky[bank][:], in0=y[bank][:], in1=damped[:])
+        def damp_bank(bank):
+            damped[bank] = keep.tile([P, BANK], F32, name="damped%d" % bank)
+            nc.scalar.mul(out=damped[bank][:], in_=y[bank][:], mul=LEAKY_SLOPE)
 
-        def add_and_store(bank):
+        def relu_bank(bank):
+            leaky[bank] = keep.tile([P, BANK], F32, name="leaky%d" % bank)
+            nc.vector.tensor_max(out=leaky[bank][:], in0=y[bank][:], in1=damped[bank][:])
+
+        def add_and_store(bank, add):
             columns = slice(bank * BANK, (bank + 1) * BANK)
-            nc.vector.tensor_add(out=leaky[bank][:], in0=leaky[bank][:], in1=p_max[:, columns])
+            add(out=leaky[bank][:], in0=leaky[bank][:], in1=p_max[:, columns])
             nc.sync.dma_start(out=out_rows[:, columns], in_=leaky[bank][:])
 
         def load_pooled(i):
@@ -179,9 +184,9 @@ def tile_gmpahead_pa_k_kernel(tc, pooled, p, Wout, out):
             )
 
         def load_p():
-            for frames in [range(FRAMES - 1), range(FRAMES - 1, FRAMES)]:
+            for frames in FRAMES_OF_LOAD:
                 part = landing.tile([P, len(frames) * C], BF16, tag="landing")
-                nc.sync.dma_start(out=part[:], in_=p_rows[:, C * frames.start : C * frames.stop])
+                nc.sync.dma_start(out=part[:], in_=p_rows[:, C * frames[0] : C * (frames[-1] + 1)])
                 for place, frame in enumerate(frames):
                     sources[("p", frame)] = part[:, C * place : C * (place + 1)]
 
@@ -207,7 +212,8 @@ def tile_gmpahead_pa_k_kernel(tc, pooled, p, Wout, out):
 
         def regroup_step(kind, *which):
             if kind == "w":
-                regroup_unit(*which)
+                regroup_on_vector(*which)
+                regroup_on_scalar(*which)
             else:
                 regroup_pooled(*which)
 
@@ -231,24 +237,54 @@ def tile_gmpahead_pa_k_kernel(tc, pooled, p, Wout, out):
                 waiting = waiting[len(ready) :]
                 for unit in ready:
                     multiply_unit(*unit)
+
+        def close_bank(bank):
+            quantise_unit(*last_units[bank])
+            multiply_unit(*last_units[bank])
+
+        def open_bank(bank):
+            for g in range(PASSES - PIECE_PASSES, PASSES - 1):
+                multiply_unit(g, bank * BANK, BANK)
+
         last_units = [(PASSES - 1, first, BANK) for first in range(0, C, BANK)]
+        last_piece = POOLED_PIECES - 1
         load(PASSES - 1)
         prepare(PASSES - 1)
+        load_pooled(last_piece)
         load_p()
-        for unit in last_units:
-            regroup_on_tensor(*unit)
         quantise_unit(*steps[-1][1:])
-        multiply_unit(*steps[-1][1:])
+        regroup_on_tensor(*last_units[0])
+        turn_pooled(last_piece)
+        regroup_on_tensor(*last_units[1])
         for unit in last_units:
-            regroup_unit(*unit)
-        for bank, unit in enumerate(last_units):
-            quantise_unit(*unit)
-            multiply_unit(*unit)
-            if bank in (1, 2):
-                take_frame(bank)
+            regroup_on_vector(*unit)
+        regroup_on_scalar(*last_units[0])
+        quantise_unit(*last_units[0])
+        regroup_on_tensor(*last_units[2])
+        regroup_pooled(last_piece)
+        quantise_pooled(last_piece)
+        regroup_on_tensor(*last_units[3])
+        open_bank(0)
+        multiply_unit(*last_units[0])
+        for bank in range(1, len(y)):
+            open_bank(bank)
+        take_frame(1)
+        regroup_on_scalar(*last_units[1])
+        close_bank(1)
+        take_frame(2)
+        regroup_on_scalar(*last_units[2])
+        damp_bank(0)
+        close_bank(2)
         relu_bank(0)
         take_frame(3)
+        add_and_store(0, nc.gpsimd.tensor_add)
+        regroup_on_scalar(*last_units[3])
+        damp_bank(1)
+        damp_bank(2)
+        close_bank(3)
+        relu_bank(1)
+        relu_bank(2)
+        damp_bank(3)
+        relu_bank(3)
         for bank in range(1, len(y)):
-            relu_bank(bank)
-        for bank in range(len(y)):
-            add_and_store(bank)
+            add_and_store(bank, nc.vector.tensor_add)

from contextlib import ExitStack

import concourse.mybir as mybir
from concourse.masks import make_identity

BF16 = mybir.dt.bfloat16
F32 = mybir.dt.float32
U32 = mybir.dt.uint32
U8 = mybir.dt.uint8
FP8X4 = mybir.dt.float8_e4m3fn_x4

P = 128
PACK = 4
K_PASS = P * PACK
K = 8192
C = 2048
PASSES = K // K_PASS
BANK = 512
HALF = C // 2
RUN = 8
ROW = PACK * C
LEAKY_SLOPE = 0.01
TENSOR_COLUMNS = {HALF: 88, BANK: 128}
VECTOR_COLUMNS = {HALF: 480, BANK: 64}
MULTIPLIED_AT_ONCE = 2
POOLED_PIECES = 4
PIECE_PASSES = PASSES // POOLED_PIECES
POOLED_BEHIND_PASS = [2, 4, 8]
FRAMES_OF_LOAD = [(0, 1), (2,), (3,)]

FLOPS = 2 * P * K * C


def regroup(copy, raw, grouped, first, stop):
    src = raw[:].rearrange("q (j c) -> q j c", j=PACK)[:, :, first:stop]
    dst = grouped[:].rearrange("q (c j) -> q c j", j=PACK)[:, first:stop, :]
    copy(
        out=dst.rearrange("q (n i) j -> q n j i", i=RUN),
        in_=src.rearrange("q j (n i) -> q n j i", i=RUN),
    )


def quantise(nc, grouped, codes, scales, first, width):
    nc.vector.quantize_mx(
        out=codes[:, first : first + width].bitcast(FP8X4),
        scales=scales[:, first : first + width],
        in_=grouped[:, PACK * first : PACK * (first + width)],
    )


def tile_gmpahead_pa_k_kernel(tc, pooled, p, Wout, out):
    nc = tc.nc
    w_passes = Wout.rearrange("n (g q j) c -> (n g) q (j c)", q=P, j=PACK)
    pooled_rows = pooled.rearrange("n b k -> (n b) k")
    p_rows = p.rearrange("n b t c -> (n b) (t c)")
    out_rows = out.rearrange("n b c -> (n b) c")

    with ExitStack() as ctx:
        ctx.enter_context(tc.manual_schedule())
        keep = ctx.enter_context(tc.tile_pool(name="keep", bufs=1))
        landing = ctx.enter_context(tc.tile_pool(name="landing", bufs=5))
        pieces = ctx.enter_context(tc.tile_pool(name="pieces", bufs=2))
        regrouped = ctx.enter_context(tc.tile_pool(name="regrouped", bufs=3))
        pooled_regrouped = ctx.enter_context(tc.tile_pool(name="pooled_regrouped", bufs=1))
        quantised = ctx.enter_context(tc.tile_pool(name="quantised", bufs=5))
        psum_y = ctx.enter_context(tc.psum_pool(name="psum_y", bufs=1))
        psum_t = ctx.enter_context(tc.psum_pool(name="psum_t", bufs=4))

        warm = keep.tile([P, 2], F32)
        nc.vector.memset(warm[:, 0:1], 0.0)
        nc.scalar.mul(out=warm[:, 1:2], in_=warm[:, 0:1], mul=LEAKY_SLOPE)
        ident = keep.tile([P, P], F32)
        make_identity(nc, ident[:])
        ident_bf16 = keep.tile([P, P], BF16)
        make_identity(nc, ident_bf16[:])

        y = [psum_y.tile([P, BANK], F32, name="y%d" % bank) for bank in range(C // BANK)]
        p_max = keep.tile([P, C], BF16)
        pooled_codes = keep.tile([P, PASSES * P], U32, align_bytes=64)
        pooled_scales = keep.tile([P, PASSES * P], U8, align_bytes=64)
        damped = {}
        leaky = {}
        sources = {}
        moved = {}
        tiles = {}

        def load(g):
            raw = landing.tile([P, ROW], BF16, tag="landing")
            nc.sync.dma_start(out=raw[:], in_=w_passes[g])
            sources[g] = raw

        def prepare(g):
            grouped = regrouped.tile([P, ROW], BF16, tag="grouped", align_bytes=64)
            codes = quantised.tile([P, C], U32, align_bytes=64)
            scales = quantised.tile([P, C], U8, align_bytes=64)
            tiles[g] = (grouped, codes, scales)

        def regroup_on_vector(g, first, width):
            regroup(nc.vector.tensor_copy, sources[g], tiles[g][0], first, first + VECTOR_COLUMNS[width])

        def regroup_on_scalar(g, first, width):
            split = first + VECTOR_COLUMNS[width]
            stop = first + width - TENSOR_COLUMNS[width]
            grouped = tiles[g][0]
            regroup(nc.scalar.copy, sources[g], grouped, split, stop)
            nc.scalar.copy(out=grouped[:, PACK * stop : PACK * (first + width)], in_=moved[(g, first)][:])

        def regroup_on_tensor(g, first, width):
            columns = TENSOR_COLUMNS[width]
            product = psum_t.tile([P, columns * PACK], BF16, tag="transit")
            stop = first + width
            rows = sources[g][:].rearrange("q (j c) -> q j c", j=PACK)
            nc.tensor.matmul(
                product[:].rearrange("q (c j) -> q j c", j=PACK),
                lhsT=ident_bf16[:],
                rhs=rows[:, :, stop - columns : stop],
                start=True,
                stop=True,
            )
            moved[(g, first)] = product

        def quantise_unit(g, first, width):
            quantise(nc, *tiles[g], first, width)

        def multiply_unit(g, first, width):
            codes, scales = tiles[g][1:]
            for start in range(first, first + width, BANK):
                nc.tensor.matmul_mx(
                    out=y[start // BANK][:],
                    lhsT=pooled_codes[:, g * P : (g + 1) * P].bitcast(FP8X4),
                    lhsT_scale=pooled_scales[:, g * P : (g + 1) * P],
                    rhs=codes[:, start : start + BANK].bitcast(FP8X4),
                    rhs_scale=scales[:, start : start + BANK],
                    start=(g == 0),
                    stop=(g == PASSES - 1),
                )

        def damp_bank(bank):
            damped[bank] = keep.tile([P, BANK], F32, name="damped%d" % bank)
            nc.scalar.mul(out=damped[bank][:], in_=y[bank][:], mul=LEAKY_SLOPE)

        def relu_bank(bank):
            leaky[bank] = keep.tile([P, BANK], F32, name="leaky%d" % bank)
            nc.vector.tensor_max(out=leaky[bank][:], in0=y[bank][:], in1=damped[bank][:])

        def add_and_store(bank, add):
            columns = slice(bank * BANK, (bank + 1) * BANK)
            add(out=leaky[bank][:], in0=leaky[bank][:], in1=p_max[:, columns])
            nc.sync.dma_start(out=out_rows[:, columns], in_=leaky[bank][:])

        def load_pooled(i):
            part = pieces.tile([P, PIECE_PASSES * K_PASS], BF16, tag="piece")
            first = i * PIECE_PASSES * K_PASS
            nc.sync.dma_start(out=part[:], in_=pooled_rows[:, first : first + PIECE_PASSES * K_PASS])
            sources[("pooled", i)] = part

        def turn_pooled(i):
            words = sources[("pooled", i)][:].bitcast(F32).rearrange("b (g q u) -> b g u q", q=P, u=2)
            banks = []
            for first in range(0, PIECE_PASSES, 2):
                turned = psum_t.tile([P, 2, 2, P], F32, tag="transit")
                for g in range(2):
                    for u in range(2):
                        nc.tensor.transpose(turned[:, g, u, :], words[:, first + g, u, :], ident[:])
                banks.append(turned)
            sources[("turned", i)] = banks

        def regroup_pooled(i):
            grouped = pooled_regrouped.tile([P, PIECE_PASSES * P * PACK], BF16, align_bytes=64)
            words = grouped[:].bitcast(F32).rearrange("q (g b u) -> q g b u", b=P, u=2)
            for bank in range(2):
                nc.scalar.copy(
                    out=words[:, 2 * bank : 2 * bank + 2],
                    in_=sources[("turned", i)][bank][:].rearrange("q g u b -> q g b u"),
                )
            tiles[("pooled", i)] = grouped

        def quantise_pooled(i):
            first = i * PIECE_PASSES * P
            nc.vector.quantize_mx(
                out=pooled_codes[:, first : first + PIECE_PASSES * P].bitcast(FP8X4),
                scales=pooled_scales[:, first : first + PIECE_PASSES * P],
                in_=tiles[("pooled", i)][:],
            )

        def load_p():
            for frames in FRAMES_OF_LOAD:
                part = landing.tile([P, len(frames) * C], BF16, tag="landing")
                nc.sync.dma_start(out=part[:], in_=p_rows[:, C * frames[0] : C * (frames[-1] + 1)])
                for place, frame in enumerate(frames):
                    sources[("p", frame)] = part[:, C * place : C * (place + 1)]

        def take_frame(frame):
            best = sources[("p", 0)] if frame == 1 else p_max[:]
            nc.vector.tensor_max(out=p_max[:], in0=best, in1=sources[("p", frame)])

        steps = []
        for g in range(PASSES - 1):
            steps.extend([("w", g, first, HALF) for first in range(0, C, HALF)])
            if g in POOLED_BEHIND_PASS:
                steps.append(("pooled", POOLED_BEHIND_PASS.index(g)))

        def load_step(kind, *which):
            if kind == "w":
                if which[1] == 0:
                    load(which[0])
                    prepare(which[0])
                regroup_on_tensor(*which)
            else:
                load_pooled(*which)
                turn_pooled(*which)

        def regroup_step(kind, *which):
            if kind == "w":
                regroup_on_vector(*which)
                regroup_on_scalar(*which)
            else:
                regroup_pooled(*which)

        waiting = []
        pooled_pieces = 0
        load_step(*steps[0])
        for step in range(len(steps)):
            if step + 1 < len(steps):
                load_step(*steps[step + 1])
            regroup_step(*steps[step])
            if step >= 1:
                kind, *which = steps[step - 1]
                if kind == "w":
                    quantise_unit(*which)
                    waiting.append(which)
                else:
                    quantise_pooled(*which)
                    pooled_pieces = which[0] + 1
                ready = [unit for unit in waiting if unit[0] < pooled_pieces * PIECE_PASSES]
                ready = ready[:MULTIPLIED_AT_ONCE]
                waiting = waiting[len(ready) :]
                for unit in ready:
                    multiply_unit(*unit)

        def close_bank(bank):
            quantise_unit(*last_units[bank])
            multiply_unit(*last_units[bank])

        def open_bank(bank):
            for g in range(PASSES - PIECE_PASSES, PASSES - 1):
                multiply_unit(g, bank * BANK, BANK)

        last_units = [(PASSES - 1, first, BANK) for first in range(0, C, BANK)]
        last_piece = POOLED_PIECES - 1
        load(PASSES - 1)
        prepare(PASSES - 1)
        load_pooled(last_piece)
        load_p()
        quantise_unit(*steps[-1][1:])
        regroup_on_tensor(*last_units[0])
        turn_pooled(last_piece)
        regroup_on_tensor(*last_units[1])
        for unit in last_units:
            regroup_on_vector(*unit)
        regroup_on_scalar(*last_units[0])
        quantise_unit(*last_units[0])
        regroup_on_tensor(*last_units[2])
        regroup_pooled(last_piece)
        quantise_pooled(last_piece)
        regroup_on_tensor(*last_units[3])
        open_bank(0)
        multiply_unit(*last_units[0])
        for bank in range(1, len(y)):
            open_bank(bank)
        take_frame(1)
        regroup_on_scalar(*last_units[1])
        close_bank(1)
        take_frame(2)
        regroup_on_scalar(*last_units[2])
        damp_bank(0)
        close_bank(2)
        relu_bank(0)
        take_frame(3)
        add_and_store(0, nc.gpsimd.tensor_add)
        regroup_on_scalar(*last_units[3])
        damp_bank(1)
        damp_bank(2)
        close_bank(3)
        relu_bank(1)
        relu_bank(2)
        damp_bank(3)
        relu_bank(3)
        for bank in range(1, len(y)):
            add_and_store(bank, nc.vector.tensor_add)
